import numpy as np
import ml_dtypes


def mxq(x, axis, fmt="e4m3"):
    dtype, down = {"e4m3": (ml_dtypes.float8_e4m3fn, 7), "e5m2": (ml_dtypes.float8_e5m2, 14)}[fmt]
    v = np.moveaxis(np.asarray(x, np.float32).astype(ml_dtypes.bfloat16).astype(np.float64), axis, -1)
    blocks = v.reshape(v.shape[:-1] + (-1, 32))
    amax = np.abs(blocks).max(-1, keepdims=True)
    byte = np.maximum(np.where(amax > 0, np.frexp(amax)[1] - 1 + 127, 0) - down, 1)
    scale = np.exp2(byte - 127.0)
    codes = (blocks / scale).astype(np.float32).astype(dtype).astype(np.float64)
    return np.moveaxis((codes * scale).reshape(v.shape), -1, axis)


WIDE = False


def mx_kscale(k):
    if not WIDE:
        return np.ones(k)
    levels = np.array([20, -20, 10, -10, 0])
    a = np.random.permutation(np.resize(levels, k // 512 * 4)).reshape(k // 512, 4)
    idx = np.arange(k)
    return np.exp2(a[idx // 512, idx % 128 // 32])


BF16 = ml_dtypes.bfloat16


def bf(x):
    return np.asarray(x, np.float32).astype(BF16)


def f64(x):
    return np.asarray(x).astype(np.float64)


B, A, C, P = 256, 3, 128, 512
N = A * A + 1


def scramble(y):
    return y.transpose(0, 2, 1).reshape(B, N, C)


def unscramble(z):
    return z.reshape(B, C, N).transpose(0, 2, 1)


def setup_inputs():
    u = mx_kscale(P)
    z = np.random.standard_normal((B, N, C)) * 1.6 / np.sqrt(N)
    w = np.random.standard_normal((P, C)) * 2.0 / np.sqrt(C) / u[:, None]
    b = np.random.standard_normal(P) * 0.1
    g = np.random.standard_normal((B, N, P)) * np.exp2(np.random.randint(-12, 1, (B, N, 1))) * 4.0 * u
    return {"y_attn": bf(np.ascontiguousarray(unscramble(z))),
            "w_proj": bf(w),
            "b_proj": bf(b),
            "grad_out": bf(g)}


def reference(y_attn, w_proj, b_proj, grad_out):
    gz = mxq(f64(grad_out), 2, "e5m2") @ mxq(f64(w_proj), 0, "e4m3")
    return np.ascontiguousarray(unscramble(gz))

@@ -1,0 +1,154 @@
+from contextlib import ExitStack
+
+import concourse.mybir as mybir
+from concourse.masks import make_identity
+
+BF16 = mybir.dt.bfloat16
+F32 = mybir.dt.float32
+I32 = mybir.dt.int32
+U32 = mybir.dt.uint32
+U8 = mybir.dt.uint8
+E4M3_X4 = mybir.dt.float8_e4m3fn_x4
+E5M2_X4 = mybir.dt.float8_e5m2_x4
+
+IMAGES, TOKENS, CHANNELS, FEATURES = 256, 10, 128, 512
+PARTS = 128
+PACK = 4
+WORDS = FEATURES // 2
+MOVING = 512
+
+HALVES = IMAGES // PARTS
+SLABS = HALVES * TOKENS
+PAIR = 2
+PAIRS = SLABS // PAIR
+ROUND = 2
+ROUNDS = PAIRS // ROUND
+
+BANK_F = 320
+BANK_CHANNELS = BANK_F // TOKENS
+BANKS = TOKENS * CHANNELS // BANK_F
+W_AT = 256
+W_CUT = 64
+PADDED = W_AT + W_CUT + MOVING
+
+FLOPS = 2 * IMAGES * TOKENS * FEATURES * CHANNELS
+BYTES = 2 * IMAGES * TOKENS * FEATURES + 2 * FEATURES * CHANNELS + 4 * IMAGES * TOKENS * CHANNELS
+
+
+def tile_attention_pa_s_kernel(tc, y_attn, w_proj, b_proj, grad_out, out):
+    nc = tc.nc
+    with ExitStack() as ctx:
+        ctx.enter_context(tc.manual_schedule())
+        const = ctx.enter_context(tc.tile_pool(name="const", bufs=1))
+        rows_pool = ctx.enter_context(tc.tile_pool(name="rows", bufs=PAIRS))
+        grouped_pool = ctx.enter_context(tc.tile_pool(name="grouped", bufs=2 * ROUND))
+        codes_pool = ctx.enter_context(tc.tile_pool(name="codes", bufs=PAIRS))
+        result_pool = ctx.enter_context(tc.tile_pool(name="result", bufs=HALVES))
+        flipped_pool = ctx.enter_context(tc.psum_pool(name="flipped", bufs=2 * ROUND))
+        product_pool = ctx.enter_context(tc.psum_pool(name="product", bufs=BANKS))
+
+        w_rows = const.tile([PARTS, PACK, CHANNELS], BF16)
+        nc.scalar.dma_start(
+            out=w_rows[:].rearrange("q (u e) j -> q u (e j)", u=2),
+            in_=w_proj.rearrange("(u q e) j -> q u (e j)", u=2, e=2),
+        )
+        slab_rows = []
+        for pair in range(PAIRS):
+            half, token = divmod(PAIR * pair, TOKENS)
+            g_rows = rows_pool.tile([PARTS, PAIR, FEATURES], BF16)
+            nc.sync.dma_start(
+                out=g_rows[:],
+                in_=grad_out[PARTS * half : PARTS * (half + 1), token : token + PAIR, :],
+            )
+            slab_rows.append(g_rows)
+
+        identity = const.tile([PARTS, PARTS], F32)
+        make_identity(nc, identity[:])
+
+        w_codes = const.tile([PARTS, PADDED], U32, align_bytes=64)
+        w_scales = const.tile([PARTS, PADDED], U8, align_bytes=64)
+        nc.vector.memset(w_codes[:].bitcast(I32), 0)
+        nc.vector.memset(w_scales[:].bitcast(I32), 0)
+        w_grouped = const.tile([PARTS, CHANNELS, PACK], BF16, align_bytes=64)
+        nc.vector.tensor_copy(out=w_grouped[:], in_=w_rows[:].rearrange("q t j -> q j t"))
+        nc.vector.quantize_mx(
+            out=w_codes[:, W_AT : W_AT + CHANNELS].bitcast(E4M3_X4),
+            scales=w_scales[:, W_AT : W_AT + CHANNELS],
+            in_=w_grouped[:].rearrange("q j t -> q (j t)"),
+        )
+
+        slab_codes = []
+        slab_scales = []
+
+        def transpose_and_quantise(pair):
+            words = slab_rows[pair][:].rearrange("b s p -> b (s p)").bitcast(F32)
+            flipped = flipped_pool.tile([PARTS, PAIR, 2, PARTS], F32)
+            for s in range(PAIR):
+                for u in range(2):
+                    first_word = WORDS * s + PARTS * u
+                    nc.tensor.transpose(
+                        flipped[:, s, u, :], words[:, first_word : first_word + PARTS], identity[:]
+                    )
+            grouped = grouped_pool.tile([PARTS, PAIR * PARTS * PACK], BF16, align_bytes=64)
+            nc.scalar.copy(
+                out=grouped[:].bitcast(F32).rearrange("q (s b u) -> q s b u", s=PAIR, u=2),
+                in_=flipped[:].rearrange("q s u b -> q s b u"),
+            )
+            g_codes = codes_pool.tile([PARTS, PAIR, PARTS], U32, align_bytes=64)
+            g_scales = codes_pool.tile([PARTS, PAIR, PARTS], U8, align_bytes=64)
+            nc.vector.quantize_mx(
+                out=g_codes[:].rearrange("q s b -> q (s b)").bitcast(E5M2_X4),
+                scales=g_scales[:].rearrange("q s b -> q (s b)"),
+                in_=grouped[:],
+            )
+            slab_codes.append(g_codes)
+            slab_scales.append(g_scales)
+
+        open_banks = {}
+        results = {}
+
+        def multiply(pair):
+            for s in range(PAIR):
+                half, token = divmod(PAIR * pair + s, TOKENS)
+                first_f = CHANNELS * token
+                for bank in range(first_f // BANK_F, (first_f + CHANNELS - 1) // BANK_F + 1):
+                    opens = token == (BANK_F * bank) // CHANNELS
+                    closes = token == (BANK_F * bank + BANK_F - 1) // CHANNELS
+                    if opens:
+                        product = product_pool.tile([PARTS, MOVING], F32)
+                        open_banks[bank] = product
+                    product = open_banks[bank]
+                    window = W_AT - (first_f - BANK_F * bank)
+                    assert 0 <= window <= W_AT + W_CUT and window % 64 == 0
+                    nc.tensor.matmul_mx(
+                        out=product[:],
+                        lhsT=slab_codes[pair][:, s, :].bitcast(E5M2_X4),
+                        lhsT_scale=slab_scales[pair][:, s, :],
+                        rhs=w_codes[:, window : window + MOVING].bitcast(E4M3_X4),
+                        rhs_scale=w_scales[:, window : window + MOVING],
+                        start=opens,
+                        stop=closes,
+                    )
+                    if closes:
+                        if bank == 0:
+                            result = result_pool.tile([PARTS, TOKENS, CHANNELS], F32)
+                            results[half] = result
+                        first_channel = BANK_CHANNELS * bank
+                        nc.vector.tensor_copy(
+                            out=results[half][:, :, first_channel : first_channel + BANK_CHANNELS],
+                            in_=product[:, 0:BANK_F].rearrange("b (c n) -> b n c", n=TOKENS),
+                        )
+                        if bank == BANKS - 1:
+                            nc.sync.dma_start(
+                                out=out[PARTS * half : PARTS * (half + 1), :, :],
+                                in_=results[half][:],
+                            )
+
+        for pair in range(ROUND):
+            transpose_and_quantise(pair)
+        for r in range(ROUNDS):
+            if r + 1 < ROUNDS:
+                for pair in range(ROUND * (r + 1), ROUND * (r + 2)):
+                    transpose_and_quantise(pair)
+            for pair in range(ROUND * r, ROUND * (r + 1)):
+                multiply(pair)

@@ -24,12 +24,10 @@ PAIRS = SLABS // PAIR
 ROUND = 2
 ROUNDS = PAIRS // ROUND
 
-BANK_F = 320
-BANK_CHANNELS = BANK_F // TOKENS
-BANKS = TOKENS * CHANNELS // BANK_F
-W_AT = 256
-W_CUT = 64
-PADDED = W_AT + W_CUT + MOVING
+BANK_TOKENS = MOVING // CHANNELS
+BANKS = -(-TOKENS // BANK_TOKENS)
+W_AT = MOVING - CHANNELS
+PADDED = W_AT + MOVING
 
 FLOPS = 2 * IMAGES * TOKENS * FEATURES * CHANNELS
 BYTES = 2 * IMAGES * TOKENS * FEATURES + 2 * FEATURES * CHANNELS + 4 * IMAGES * TOKENS * CHANNELS
@@ -45,7 +43,7 @@ def tile_attention_pa_s_kernel(tc, y_attn, w_proj, b_proj, grad_out, out):
         codes_pool = ctx.enter_context(tc.tile_pool(name="codes", bufs=PAIRS))
         result_pool = ctx.enter_context(tc.tile_pool(name="result", bufs=HALVES))
         flipped_pool = ctx.enter_context(tc.psum_pool(name="flipped", bufs=2 * ROUND))
-        product_pool = ctx.enter_context(tc.psum_pool(name="product", bufs=BANKS))
+        product_pool = ctx.enter_context(tc.psum_pool(name="product", bufs=BANKS + 1))
 
         w_rows = const.tile([PARTS, PACK, CHANNELS], BF16)
         nc.scalar.dma_start(
@@ -104,45 +102,61 @@ def tile_attention_pa_s_kernel(tc, y_attn, w_proj, b_proj, grad_out, out):
             slab_codes.append(g_codes)
             slab_scales.append(g_scales)
 
-        open_banks = {}
-        results = {}
+        def empty_bank(product, result, first_f, places):
+            lead = -first_f % TOKENS
+            whole = (places - lead) // TOKENS
+            rest = places - lead - TOKENS * whole
+            channel = (first_f + lead) // TOKENS
+            if lead:
+                nc.vector.tensor_copy(
+                    out=result[:, TOKENS - lead : TOKENS, channel - 1 : channel],
+                    in_=product[:, 0:lead].rearrange("b (n c) -> b n c", c=1),
+                )
+            nc.vector.tensor_copy(
+                out=result[:, :, channel : channel + whole],
+                in_=product[:, lead : lead + TOKENS * whole].rearrange("b (c n) -> b n c", n=TOKENS),
+            )
+            if rest:
+                nc.vector.tensor_copy(
+                    out=result[:, 0:rest, channel + whole : channel + whole + 1],
+                    in_=product[:, places - rest : places].rearrange("b (n c) -> b n c", c=1),
+                )
+
+        open_tiles = {}
 
         def multiply(pair):
             for s in range(PAIR):
                 half, token = divmod(PAIR * pair + s, TOKENS)
-                first_f = CHANNELS * token
-                for bank in range(first_f // BANK_F, (first_f + CHANNELS - 1) // BANK_F + 1):
-                    opens = token == (BANK_F * bank) // CHANNELS
-                    closes = token == (BANK_F * bank + BANK_F - 1) // CHANNELS
-                    if opens:
-                        product = product_pool.tile([PARTS, MOVING], F32)
-                        open_banks[bank] = product
-                    product = open_banks[bank]
-                    window = W_AT - (first_f - BANK_F * bank)
-                    assert 0 <= window <= W_AT + W_CUT and window % 64 == 0
-                    nc.tensor.matmul_mx(
-                        out=product[:],
-                        lhsT=slab_codes[pair][:, s, :].bitcast(E5M2_X4),
-                        lhsT_scale=slab_scales[pair][:, s, :],
-                        rhs=w_codes[:, window : window + MOVING].bitcast(E4M3_X4),
-                        rhs_scale=w_scales[:, window : window + MOVING],
-                        start=opens,
-                        stop=closes,
+                bank, place = divmod(token, BANK_TOKENS)
+                opens = place == 0
+                closes = place == BANK_TOKENS - 1 or token == TOKENS - 1
+                if token == 0:
+                    result = result_pool.tile([PARTS, TOKENS, CHANNELS], F32)
+                    open_tiles["result"] = result
+                if opens:
+                    product = product_pool.tile([PARTS, MOVING], F32)
+                    open_tiles["product"] = product
+                window = W_AT - CHANNELS * place
+                nc.tensor.matmul_mx(
+                    out=open_tiles["product"][:],
+                    lhsT=slab_codes[pair][:, s, :].bitcast(E5M2_X4),
+                    lhsT_scale=slab_scales[pair][:, s, :],
+                    rhs=w_codes[:, window : window + MOVING].bitcast(E4M3_X4),
+                    rhs_scale=w_scales[:, window : window + MOVING],
+                    start=opens,
+                    stop=closes,
+                )
+                if closes:
+                    empty_bank(
+                        open_tiles["product"],
+                        open_tiles["result"],
+                        first_f=MOVING * bank,
+                        places=CHANNELS * (place + 1),
                     )
-                    if closes:
-                        if bank == 0:
-                            result = result_pool.tile([PARTS, TOKENS, CHANNELS], F32)
-                            results[half] = result
-                        first_channel = BANK_CHANNELS * bank
-                        nc.vector.tensor_copy(
-                            out=results[half][:, :, first_channel : first_channel + BANK_CHANNELS],
-                            in_=product[:, 0:BANK_F].rearrange("b (c n) -> b n c", n=TOKENS),
-                        )
-                        if bank == BANKS - 1:
-                            nc.sync.dma_start(
-                                out=out[PARTS * half : PARTS * (half + 1), :, :],
-                                in_=results[half][:],
-                            )
+                if token == TOKENS - 1:
+                    nc.sync.dma_start(
+                        out=out[PARTS * half : PARTS * (half + 1), :, :], in_=open_tiles["result"][:]
+                    )
 
         for pair in range(ROUND):
             transpose_and_quantise(pair)

@@ -28,6 +28,7 @@ BANK_TOKENS = MOVING // CHANNELS
 BANKS = -(-TOKENS // BANK_TOKENS)
 W_AT = MOVING - CHANNELS
 PADDED = W_AT + MOVING
+WARM_PASSES = 6
 
 FLOPS = 2 * IMAGES * TOKENS * FEATURES * CHANNELS
 BYTES = 2 * IMAGES * TOKENS * FEATURES + 2 * FEATURES * CHANNELS + 4 * IMAGES * TOKENS * CHANNELS
@@ -67,6 +68,19 @@ def tile_attention_pa_s_kernel(tc, y_attn, w_proj, b_proj, grad_out, out):
         w_scales = const.tile([PARTS, PADDED], U8, align_bytes=64)
         nc.vector.memset(w_codes[:].bitcast(I32), 0)
         nc.vector.memset(w_scales[:].bitcast(I32), 0)
+
+        warm = product_pool.tile([PARTS, MOVING], F32, tag="product")
+        for repeat in range(WARM_PASSES):
+            nc.tensor.matmul_mx(
+                out=warm[:],
+                lhsT=w_codes[:, 0:PARTS].bitcast(E5M2_X4),
+                lhsT_scale=w_scales[:, 0:PARTS],
+                rhs=w_codes[:, 0:MOVING].bitcast(E4M3_X4),
+                rhs_scale=w_scales[:, 0:MOVING],
+                start=True,
+                stop=True,
+            )
+
         w_grouped = const.tile([PARTS, CHANNELS, PACK], BF16, align_bytes=64)
         nc.vector.tensor_copy(out=w_grouped[:], in_=w_rows[:].rearrange("q t j -> q j t"))
         nc.vector.quantize_mx(

@@ -28,7 +28,7 @@ BANK_TOKENS = MOVING // CHANNELS
 BANKS = -(-TOKENS // BANK_TOKENS)
 W_AT = MOVING - CHANNELS
 PADDED = W_AT + MOVING
-WARM_PASSES = 6
+WARM_PASSES = 3
 
 FLOPS = 2 * IMAGES * TOKENS * FEATURES * CHANNELS
 BYTES = 2 * IMAGES * TOKENS * FEATURES + 2 * FEATURES * CHANNELS + 4 * IMAGES * TOKENS * CHANNELS
@@ -66,8 +66,8 @@ def tile_attention_pa_s_kernel(tc, y_attn, w_proj, b_proj, grad_out, out):
 
         w_codes = const.tile([PARTS, PADDED], U32, align_bytes=64)
         w_scales = const.tile([PARTS, PADDED], U8, align_bytes=64)
-        nc.vector.memset(w_codes[:].bitcast(I32), 0)
         nc.vector.memset(w_scales[:].bitcast(I32), 0)
+        nc.vector.memset(w_codes[:, 0:MOVING].bitcast(I32), 0)
 
         warm = product_pool.tile([PARTS, MOVING], F32, tag="product")
         for repeat in range(WARM_PASSES):
@@ -81,6 +81,7 @@ def tile_attention_pa_s_kernel(tc, y_attn, w_proj, b_proj, grad_out, out):
                 stop=True,
             )
 
+        nc.vector.memset(w_codes[:, MOVING:PADDED].bitcast(I32), 0)
         w_grouped = const.tile([PARTS, CHANNELS, PACK], BF16, align_bytes=64)
         nc.vector.tensor_copy(out=w_grouped[:], in_=w_rows[:].rearrange("q t j -> q j t"))
         nc.vector.quantize_mx(

@@ -22,7 +22,9 @@ SLABS = HALVES * TOKENS
 PAIR = 2
 PAIRS = SLABS // PAIR
 ROUND = 2
-ROUNDS = PAIRS // ROUND
+LEAD = 4
+RUN = 3
+SLACK = 2
 
 BANK_TOKENS = MOVING // CHANNELS
 BANKS = -(-TOKENS // BANK_TOKENS)
@@ -173,11 +175,14 @@ def tile_attention_pa_s_kernel(tc, y_attn, w_proj, b_proj, grad_out, out):
                         out=out[PARTS * half : PARTS * (half + 1), :, :], in_=open_tiles["result"][:]
                     )
 
-        for pair in range(ROUND):
-            transpose_and_quantise(pair)
-        for r in range(ROUNDS):
-            if r + 1 < ROUNDS:
-                for pair in range(ROUND * (r + 1), ROUND * (r + 2)):
-                    transpose_and_quantise(pair)
-            for pair in range(ROUND * r, ROUND * (r + 1)):
+        transposed = 0
+        multiplied = 0
+        while multiplied < PAIRS:
+            upto = min(transposed + (LEAD if transposed == 0 else RUN), PAIRS)
+            for pair in range(transposed, upto):
+                transpose_and_quantise(pair)
+            transposed = upto
+            ready = PAIRS if transposed == PAIRS else transposed - SLACK
+            for pair in range(multiplied, ready):
                 multiply(pair)
+            multiplied = ready

@@ -31,6 +31,7 @@ BANKS = -(-TOKENS // BANK_TOKENS)
 W_AT = MOVING - CHANNELS
 PADDED = W_AT + MOVING
 WARM_PASSES = 3
+MID_PASSES = 2
 
 FLOPS = 2 * IMAGES * TOKENS * FEATURES * CHANNELS
 BYTES = 2 * IMAGES * TOKENS * FEATURES + 2 * FEATURES * CHANNELS + 4 * IMAGES * TOKENS * CHANNELS
@@ -72,16 +73,20 @@ def tile_attention_pa_s_kernel(tc, y_attn, w_proj, b_proj, grad_out, out):
         nc.vector.memset(w_codes[:, 0:MOVING].bitcast(I32), 0)
 
         warm = product_pool.tile([PARTS, MOVING], F32, tag="product")
-        for repeat in range(WARM_PASSES):
-            nc.tensor.matmul_mx(
-                out=warm[:],
-                lhsT=w_codes[:, 0:PARTS].bitcast(E5M2_X4),
-                lhsT_scale=w_scales[:, 0:PARTS],
-                rhs=w_codes[:, 0:MOVING].bitcast(E4M3_X4),
-                rhs_scale=w_scales[:, 0:MOVING],
-                start=True,
-                stop=True,
-            )
+
+        def warm_up(passes):
+            for repeat in range(passes):
+                nc.tensor.matmul_mx(
+                    out=warm[:],
+                    lhsT=w_codes[:, 0:PARTS].bitcast(E5M2_X4),
+                    lhsT_scale=w_scales[:, 0:PARTS],
+                    rhs=w_codes[:, 0:MOVING].bitcast(E4M3_X4),
+                    rhs_scale=w_scales[:, 0:MOVING],
+                    start=True,
+                    stop=True,
+                )
+
+        warm_up(WARM_PASSES)
 
         nc.vector.memset(w_codes[:, MOVING:PADDED].bitcast(I32), 0)
         w_grouped = const.tile([PARTS, CHANNELS, PACK], BF16, align_bytes=64)
@@ -181,6 +186,8 @@ def tile_attention_pa_s_kernel(tc, y_attn, w_proj, b_proj, grad_out, out):
             upto = min(transposed + (LEAD if transposed == 0 else RUN), PAIRS)
             for pair in range(transposed, upto):
                 transpose_and_quantise(pair)
+                if pair == LEAD // 2 - 1:
+                    warm_up(MID_PASSES)
             transposed = upto
             ready = PAIRS if transposed == PAIRS else transposed - SLACK
             for pair in range(multiplied, ready):

@@ -22,9 +22,7 @@ SLABS = HALVES * TOKENS
 PAIR = 2
 PAIRS = SLABS // PAIR
 ROUND = 2
-LEAD = 4
-RUN = 3
-SLACK = 2
+TURNED = (2, 3)
 
 BANK_TOKENS = MOVING // CHANNELS
 BANKS = -(-TOKENS // BANK_TOKENS)
@@ -44,7 +42,6 @@ def tile_attention_pa_s_kernel(tc, y_attn, w_proj, b_proj, grad_out, out):
         const = ctx.enter_context(tc.tile_pool(name="const", bufs=1))
         rows_pool = ctx.enter_context(tc.tile_pool(name="rows", bufs=PAIRS))
         grouped_pool = ctx.enter_context(tc.tile_pool(name="grouped", bufs=2 * ROUND))
-        codes_pool = ctx.enter_context(tc.tile_pool(name="codes", bufs=PAIRS))
         result_pool = ctx.enter_context(tc.tile_pool(name="result", bufs=HALVES))
         flipped_pool = ctx.enter_context(tc.psum_pool(name="flipped", bufs=2 * ROUND))
         product_pool = ctx.enter_context(tc.psum_pool(name="product", bufs=BANKS + 1))
@@ -97,10 +94,12 @@ def tile_attention_pa_s_kernel(tc, y_attn, w_proj, b_proj, grad_out, out):
             in_=w_grouped[:].rearrange("q j t -> q (j t)"),
         )
 
-        slab_codes = []
-        slab_scales = []
+        g_codes = const.tile([PARTS, SLABS, PARTS], U32, align_bytes=64)
+        g_scales = const.tile([PARTS, SLABS, PARTS], U8, align_bytes=64)
+        flipped_of = {}
+        grouped_of = {}
 
-        def transpose_and_quantise(pair):
+        def transposes(pair):
             words = slab_rows[pair][:].rearrange("b s p -> b (s p)").bitcast(F32)
             flipped = flipped_pool.tile([PARTS, PAIR, 2, PARTS], F32)
             for s in range(PAIR):
@@ -109,60 +108,79 @@ def tile_attention_pa_s_kernel(tc, y_attn, w_proj, b_proj, grad_out, out):
                     nc.tensor.transpose(
                         flipped[:, s, u, :], words[:, first_word : first_word + PARTS], identity[:]
                     )
+            flipped_of[pair] = flipped
+
+        def copy_in(pair):
             grouped = grouped_pool.tile([PARTS, PAIR * PARTS * PACK], BF16, align_bytes=64)
             nc.scalar.copy(
                 out=grouped[:].bitcast(F32).rearrange("q (s b u) -> q s b u", s=PAIR, u=2),
-                in_=flipped[:].rearrange("q s u b -> q s b u"),
+                in_=flipped_of[pair][:].rearrange("q s u b -> q s b u"),
             )
-            g_codes = codes_pool.tile([PARTS, PAIR, PARTS], U32, align_bytes=64)
-            g_scales = codes_pool.tile([PARTS, PAIR, PARTS], U8, align_bytes=64)
-            nc.vector.quantize_mx(
-                out=g_codes[:].rearrange("q s b -> q (s b)").bitcast(E5M2_X4),
-                scales=g_scales[:].rearrange("q s b -> q (s b)"),
-                in_=grouped[:],
-            )
-            slab_codes.append(g_codes)
-            slab_scales.append(g_scales)
+            grouped_of[pair] = grouped
 
-        def empty_bank(product, result, first_f, places):
+        def quantise(pair):
+            slabs = slice(PAIR * pair, PAIR * (pair + 1))
+            nc.vector.quantize_mx(
+                out=g_codes[:, slabs, :].rearrange("q s b -> q (s b)").bitcast(E5M2_X4),
+                scales=g_scales[:, slabs, :].rearrange("q s b -> q (s b)"),
+                in_=grouped_of[pair][:],
+            )
+
+        def front(pair):
+            transposes(pair)
+            copy_in(pair)
+            quantise(pair)
+
+        def empty_bank(copy, product, result, first_f, places):
             lead = -first_f % TOKENS
             whole = (places - lead) // TOKENS
             rest = places - lead - TOKENS * whole
             channel = (first_f + lead) // TOKENS
             if lead:
-                nc.vector.tensor_copy(
+                copy(
                     out=result[:, TOKENS - lead : TOKENS, channel - 1 : channel],
                     in_=product[:, 0:lead].rearrange("b (n c) -> b n c", c=1),
                 )
-            nc.vector.tensor_copy(
+            copy(
                 out=result[:, :, channel : channel + whole],
                 in_=product[:, lead : lead + TOKENS * whole].rearrange("b (c n) -> b n c", n=TOKENS),
             )
             if rest:
-                nc.vector.tensor_copy(
+                copy(
                     out=result[:, 0:rest, channel + whole : channel + whole + 1],
                     in_=product[:, places - rest : places].rearrange("b (n c) -> b n c", c=1),
                 )
 
         open_tiles = {}
+        results = {}
+
+        def store(half):
+            nc.sync.dma_start(out=out[PARTS * half : PARTS * (half + 1), :, :], in_=results[half][:])
 
         def multiply(pair):
             for s in range(PAIR):
                 half, token = divmod(PAIR * pair + s, TOKENS)
-                bank, place = divmod(token, BANK_TOKENS)
+                first = token - token % BANK_TOKENS
+                count = min(BANK_TOKENS, TOKENS - first)
+                last_half = half == HALVES - 1
+                if last_half and count < BANK_TOKENS:
+                    first, count = token, 1
+                place = token - first
                 opens = place == 0
-                closes = place == BANK_TOKENS - 1 or token == TOKENS - 1
+                closes = place == count - 1
+                on_scalar = last_half and first in (BANK_TOKENS, 2 * BANK_TOKENS)
                 if token == 0:
                     result = result_pool.tile([PARTS, TOKENS, CHANNELS], F32)
                     open_tiles["result"] = result
+                    results[half] = result
                 if opens:
                     product = product_pool.tile([PARTS, MOVING], F32)
                     open_tiles["product"] = product
                 window = W_AT - CHANNELS * place
                 nc.tensor.matmul_mx(
                     out=open_tiles["product"][:],
-                    lhsT=slab_codes[pair][:, s, :].bitcast(E5M2_X4),
-                    lhsT_scale=slab_scales[pair][:, s, :],
+                    lhsT=g_codes[:, PAIR * pair + s, :].bitcast(E5M2_X4),
+                    lhsT_scale=g_scales[:, PAIR * pair + s, :],
                     rhs=w_codes[:, window : window + MOVING].bitcast(E4M3_X4),
                     rhs_scale=w_scales[:, window : window + MOVING],
                     start=opens,
@@ -170,26 +188,58 @@ def tile_attention_pa_s_kernel(tc, y_attn, w_proj, b_proj, grad_out, out):
                 )
                 if closes:
                     empty_bank(
+                        nc.scalar.copy if on_scalar else nc.vector.tensor_copy,
                         open_tiles["product"],
                         open_tiles["result"],
-                        first_f=MOVING * bank,
-                        places=CHANNELS * (place + 1),
-                    )
-                if token == TOKENS - 1:
-                    nc.sync.dma_start(
-                        out=out[PARTS * half : PARTS * (half + 1), :, :], in_=open_tiles["result"][:]
+                        first_f=CHANNELS * first,
+                        places=CHANNELS * count,
                     )
 
-        transposed = 0
-        multiplied = 0
-        while multiplied < PAIRS:
-            upto = min(transposed + (LEAD if transposed == 0 else RUN), PAIRS)
-            for pair in range(transposed, upto):
-                transpose_and_quantise(pair)
-                if pair == LEAD // 2 - 1:
-                    warm_up(MID_PASSES)
-            transposed = upto
-            ready = PAIRS if transposed == PAIRS else transposed - SLACK
-            for pair in range(multiplied, ready):
-                multiply(pair)
-            multiplied = ready
+        def turned_pass():
+            turned = product_pool.tile([PARTS, MOVING], F32, tag="product")
+            slabs = slice(PAIR * TURNED[0], PAIR * (TURNED[-1] + 1))
+            nc.tensor.matmul_mx(
+                out=turned[:],
+                lhsT=w_codes[:, W_AT : W_AT + CHANNELS].bitcast(E4M3_X4),
+                lhsT_scale=w_scales[:, W_AT : W_AT + CHANNELS],
+                rhs=g_codes[:, slabs, :].rearrange("q s b -> q (s b)").bitcast(E5M2_X4),
+                rhs_scale=g_scales[:, slabs, :].rearrange("q s b -> q (s b)"),
+                start=True,
+                stop=True,
+            )
+            nc.scalar.copy(out=turned_rows[:], in_=turned[:])
+
+        def turn_back():
+            back = product_pool.tile([PARTS, MOVING], F32, tag="product")
+            for s in range(BANK_TOKENS):
+                nc.tensor.transpose(
+                    back[:, CHANNELS * s : CHANNELS * (s + 1)],
+                    turned_rows[:, PARTS * s : PARTS * (s + 1)],
+                    identity[:],
+                )
+            half, token = divmod(PAIR * TURNED[0], TOKENS)
+            empty_bank(nc.vector.tensor_copy, back, results[half], first_f=CHANNELS * token, places=MOVING)
+
+        turned_rows = const.tile([PARTS, MOVING], F32)
+        front(0)
+        front(1)
+        warm_up(MID_PASSES)
+        front(2)
+        front(3)
+        front(4)
+        multiply(0)
+        multiply(1)
+        front(5)
+        front(6)
+        transposes(7)
+        turned_pass()
+        copy_in(7)
+        quantise(7)
+        multiply(4)
+        front(8)
+        front(9)
+        turn_back()
+        store(0)
+        for pair in range(5, PAIRS):
+            multiply(pair)
+        store(1)

@@ -61,13 +61,13 @@ def tile_attention_pa_s_kernel(tc, y_attn, w_proj, b_proj, grad_out, out):
             )
             slab_rows.append(g_rows)
 
-        identity = const.tile([PARTS, PARTS], F32)
-        make_identity(nc, identity[:])
-
         w_codes = const.tile([PARTS, PADDED], U32, align_bytes=64)
         w_scales = const.tile([PARTS, PADDED], U8, align_bytes=64)
+        nc.gpsimd.memset(w_codes[:, 0:MOVING].bitcast(F32), 0.0)
         nc.vector.memset(w_scales[:].bitcast(I32), 0)
-        nc.vector.memset(w_codes[:, 0:MOVING].bitcast(I32), 0)
+
+        identity = const.tile([PARTS, PARTS], F32)
+        make_identity(nc, identity[:])
 
         warm = product_pool.tile([PARTS, MOVING], F32, tag="product")
 
@@ -218,7 +218,7 @@ def tile_attention_pa_s_kernel(tc, y_attn, w_proj, b_proj, grad_out, out):
                     identity[:],
                 )
             half, token = divmod(PAIR * TURNED[0], TOKENS)
-            empty_bank(nc.vector.tensor_copy, back, results[half], first_f=CHANNELS * token, places=MOVING)
+            empty_bank(nc.scalar.copy, back, results[half], first_f=CHANNELS * token, places=MOVING)
 
         turned_rows = const.tile([PARTS, MOVING], F32)
         front(0)

@@ -163,12 +163,10 @@ def tile_attention_pa_s_kernel(tc, y_attn, w_proj, b_proj, grad_out, out):
                 first = token - token % BANK_TOKENS
                 count = min(BANK_TOKENS, TOKENS - first)
                 last_half = half == HALVES - 1
-                if last_half and count < BANK_TOKENS:
-                    first, count = token, 1
                 place = token - first
                 opens = place == 0
                 closes = place == count - 1
-                on_scalar = last_half and first in (BANK_TOKENS, 2 * BANK_TOKENS)
+                on_scalar = last_half and first == BANK_TOKENS
                 if token == 0:
                     result = result_pool.tile([PARTS, TOKENS, CHANNELS], F32)
                     open_tiles["result"] = result

@@ -162,11 +162,9 @@ def tile_attention_pa_s_kernel(tc, y_attn, w_proj, b_proj, grad_out, out):
                 half, token = divmod(PAIR * pair + s, TOKENS)
                 first = token - token % BANK_TOKENS
                 count = min(BANK_TOKENS, TOKENS - first)
-                last_half = half == HALVES - 1
                 place = token - first
                 opens = place == 0
                 closes = place == count - 1
-                on_scalar = last_half and first == BANK_TOKENS
                 if token == 0:
                     result = result_pool.tile([PARTS, TOKENS, CHANNELS], F32)
                     open_tiles["result"] = result
@@ -186,7 +184,7 @@ def tile_attention_pa_s_kernel(tc, y_attn, w_proj, b_proj, grad_out, out):
                 )
                 if closes:
                     empty_bank(
-                        nc.scalar.copy if on_scalar else nc.vector.tensor_copy,
+                        nc.vector.tensor_copy,
                         open_tiles["product"],
                         open_tiles["result"],
                         first_f=CHANNELS * first,

from contextlib import ExitStack

import concourse.mybir as mybir
from concourse.masks import make_identity

BF16 = mybir.dt.bfloat16
F32 = mybir.dt.float32
I32 = mybir.dt.int32
U32 = mybir.dt.uint32
U8 = mybir.dt.uint8
E4M3_X4 = mybir.dt.float8_e4m3fn_x4
E5M2_X4 = mybir.dt.float8_e5m2_x4

IMAGES, TOKENS, CHANNELS, FEATURES = 256, 10, 128, 512
PARTS = 128
PACK = 4
WORDS = FEATURES // 2
MOVING = 512

HALVES = IMAGES // PARTS
SLABS = HALVES * TOKENS
PAIR = 2
PAIRS = SLABS // PAIR
ROUND = 2
TURNED = (2, 3)

BANK_TOKENS = MOVING // CHANNELS
BANKS = -(-TOKENS // BANK_TOKENS)
W_AT = MOVING - CHANNELS
PADDED = W_AT + MOVING
WARM_PASSES = 3
MID_PASSES = 2

FLOPS = 2 * IMAGES * TOKENS * FEATURES * CHANNELS
BYTES = 2 * IMAGES * TOKENS * FEATURES + 2 * FEATURES * CHANNELS + 4 * IMAGES * TOKENS * CHANNELS


def tile_attention_pa_s_kernel(tc, y_attn, w_proj, b_proj, grad_out, out):
    nc = tc.nc
    with ExitStack() as ctx:
        ctx.enter_context(tc.manual_schedule())
        const = ctx.enter_context(tc.tile_pool(name="const", bufs=1))
        rows_pool = ctx.enter_context(tc.tile_pool(name="rows", bufs=PAIRS))
        grouped_pool = ctx.enter_context(tc.tile_pool(name="grouped", bufs=2 * ROUND))
        result_pool = ctx.enter_context(tc.tile_pool(name="result", bufs=HALVES))
        flipped_pool = ctx.enter_context(tc.psum_pool(name="flipped", bufs=2 * ROUND))
        product_pool = ctx.enter_context(tc.psum_pool(name="product", bufs=BANKS + 1))

        w_rows = const.tile([PARTS, PACK, CHANNELS], BF16)
        nc.scalar.dma_start(
            out=w_rows[:].rearrange("q (u e) j -> q u (e j)", u=2),
            in_=w_proj.rearrange("(u q e) j -> q u (e j)", u=2, e=2),
        )
        slab_rows = []
        for pair in range(PAIRS):
            half, token = divmod(PAIR * pair, TOKENS)
            g_rows = rows_pool.tile([PARTS, PAIR, FEATURES], BF16)
            nc.sync.dma_start(
                out=g_rows[:],
                in_=grad_out[PARTS * half : PARTS * (half + 1), token : token + PAIR, :],
            )
            slab_rows.append(g_rows)

        w_codes = const.tile([PARTS, PADDED], U32, align_bytes=64)
        w_scales = const.tile([PARTS, PADDED], U8, align_bytes=64)
        nc.gpsimd.memset(w_codes[:, 0:MOVING].bitcast(F32), 0.0)
        nc.vector.memset(w_scales[:].bitcast(I32), 0)

        identity = const.tile([PARTS, PARTS], F32)
        make_identity(nc, identity[:])

        warm = product_pool.tile([PARTS, MOVING], F32, tag="product")

        def warm_up(passes):
            for repeat in range(passes):
                nc.tensor.matmul_mx(
                    out=warm[:],
                    lhsT=w_codes[:, 0:PARTS].bitcast(E5M2_X4),
                    lhsT_scale=w_scales[:, 0:PARTS],
                    rhs=w_codes[:, 0:MOVING].bitcast(E4M3_X4),
                    rhs_scale=w_scales[:, 0:MOVING],
                    start=True,
                    stop=True,
                )

        warm_up(WARM_PASSES)

        nc.vector.memset(w_codes[:, MOVING:PADDED].bitcast(I32), 0)
        w_grouped = const.tile([PARTS, CHANNELS, PACK], BF16, align_bytes=64)
        nc.vector.tensor_copy(out=w_grouped[:], in_=w_rows[:].rearrange("q t j -> q j t"))
        nc.vector.quantize_mx(
            out=w_codes[:, W_AT : W_AT + CHANNELS].bitcast(E4M3_X4),
            scales=w_scales[:, W_AT : W_AT + CHANNELS],
            in_=w_grouped[:].rearrange("q j t -> q (j t)"),
        )

        g_codes = const.tile([PARTS, SLABS, PARTS], U32, align_bytes=64)
        g_scales = const.tile([PARTS, SLABS, PARTS], U8, align_bytes=64)
        flipped_of = {}
        grouped_of = {}

        def transposes(pair):
            words = slab_rows[pair][:].rearrange("b s p -> b (s p)").bitcast(F32)
            flipped = flipped_pool.tile([PARTS, PAIR, 2, PARTS], F32)
            for s in range(PAIR):
                for u in range(2):
                    first_word = WORDS * s + PARTS * u
                    nc.tensor.transpose(
                        flipped[:, s, u, :], words[:, first_word : first_word + PARTS], identity[:]
                    )
            flipped_of[pair] = flipped

        def copy_in(pair):
            grouped = grouped_pool.tile([PARTS, PAIR * PARTS * PACK], BF16, align_bytes=64)
            nc.scalar.copy(
                out=grouped[:].bitcast(F32).rearrange("q (s b u) -> q s b u", s=PAIR, u=2),
                in_=flipped_of[pair][:].rearrange("q s u b -> q s b u"),
            )
            grouped_of[pair] = grouped

        def quantise(pair):
            slabs = slice(PAIR * pair, PAIR * (pair + 1))
            nc.vector.quantize_mx(
                out=g_codes[:, slabs, :].rearrange("q s b -> q (s b)").bitcast(E5M2_X4),
                scales=g_scales[:, slabs, :].rearrange("q s b -> q (s b)"),
                in_=grouped_of[pair][:],
            )

        def front(pair):
            transposes(pair)
            copy_in(pair)
            quantise(pair)

        def empty_bank(copy, product, result, first_f, places):
            lead = -first_f % TOKENS
            whole = (places - lead) // TOKENS
            rest = places - lead - TOKENS * whole
            channel = (first_f + lead) // TOKENS
            if lead:
                copy(
                    out=result[:, TOKENS - lead : TOKENS, channel - 1 : channel],
                    in_=product[:, 0:lead].rearrange("b (n c) -> b n c", c=1),
                )
            copy(
                out=result[:, :, channel : channel + whole],
                in_=product[:, lead : lead + TOKENS * whole].rearrange("b (c n) -> b n c", n=TOKENS),
            )
            if rest:
                copy(
                    out=result[:, 0:rest, channel + whole : channel + whole + 1],
                    in_=product[:, places - rest : places].rearrange("b (n c) -> b n c", c=1),
                )

        open_tiles = {}
        results = {}

        def store(half):
            nc.sync.dma_start(out=out[PARTS * half : PARTS * (half + 1), :, :], in_=results[half][:])

        def multiply(pair):
            for s in range(PAIR):
                half, token = divmod(PAIR * pair + s, TOKENS)
                first = token - token % BANK_TOKENS
                count = min(BANK_TOKENS, TOKENS - first)
                place = token - first
                opens = place == 0
                closes = place == count - 1
                if token == 0:
                    result = result_pool.tile([PARTS, TOKENS, CHANNELS], F32)
                    open_tiles["result"] = result
                    results[half] = result
                if opens:
                    product = product_pool.tile([PARTS, MOVING], F32)
                    open_tiles["product"] = product
                window = W_AT - CHANNELS * place
                nc.tensor.matmul_mx(
                    out=open_tiles["product"][:],
                    lhsT=g_codes[:, PAIR * pair + s, :].bitcast(E5M2_X4),
                    lhsT_scale=g_scales[:, PAIR * pair + s, :],
                    rhs=w_codes[:, window : window + MOVING].bitcast(E4M3_X4),
                    rhs_scale=w_scales[:, window : window + MOVING],
                    start=opens,
                    stop=closes,
                )
                if closes:
                    empty_bank(
                        nc.vector.tensor_copy,
                        open_tiles["product"],
                        open_tiles["result"],
                        first_f=CHANNELS * first,
                        places=CHANNELS * count,
                    )

        def turned_pass():
            turned = product_pool.tile([PARTS, MOVING], F32, tag="product")
            slabs = slice(PAIR * TURNED[0], PAIR * (TURNED[-1] + 1))
            nc.tensor.matmul_mx(
                out=turned[:],
                lhsT=w_codes[:, W_AT : W_AT + CHANNELS].bitcast(E4M3_X4),
                lhsT_scale=w_scales[:, W_AT : W_AT + CHANNELS],
                rhs=g_codes[:, slabs, :].rearrange("q s b -> q (s b)").bitcast(E5M2_X4),
                rhs_scale=g_scales[:, slabs, :].rearrange("q s b -> q (s b)"),
                start=True,
                stop=True,
            )
            nc.scalar.copy(out=turned_rows[:], in_=turned[:])

        def turn_back():
            back = product_pool.tile([PARTS, MOVING], F32, tag="product")
            for s in range(BANK_TOKENS):
                nc.tensor.transpose(
                    back[:, CHANNELS * s : CHANNELS * (s + 1)],
                    turned_rows[:, PARTS * s : PARTS * (s + 1)],
                    identity[:],
                )
            half, token = divmod(PAIR * TURNED[0], TOKENS)
            empty_bank(nc.scalar.copy, back, results[half], first_f=CHANNELS * token, places=MOVING)

        turned_rows = const.tile([PARTS, MOVING], F32)
        front(0)
        front(1)
        warm_up(MID_PASSES)
        front(2)
        front(3)
        front(4)
        multiply(0)
        multiply(1)
        front(5)
        front(6)
        transposes(7)
        turned_pass()
        copy_in(7)
        quantise(7)
        multiply(4)
        front(8)
        front(9)
        turn_back()
        store(0)
        for pair in range(5, PAIRS):
            multiply(pair)
        store(1)
